import numpy as np
import ml_dtypes


def mxq(x, axis, fmt="e4m3"):
    dtype, down = {"e4m3": (ml_dtypes.float8_e4m3fn, 7), "e5m2": (ml_dtypes.float8_e5m2, 14)}[fmt]
    v = np.moveaxis(np.asarray(x, np.float32).astype(ml_dtypes.bfloat16).astype(np.float64), axis, -1)
    blocks = v.reshape(v.shape[:-1] + (-1, 32))
    amax = np.abs(blocks).max(-1, keepdims=True)
    byte = np.maximum(np.where(amax > 0, np.frexp(amax)[1] - 1 + 127, 0) - down, 1)
    scale = np.exp2(byte - 127.0)
    codes = (blocks / scale).astype(np.float32).astype(dtype).astype(np.float64)
    return np.moveaxis((codes * scale).reshape(v.shape), -1, axis)


WIDE = False


def mx_kscale(k):
    if not WIDE:
        return np.ones(k)
    levels = np.array([10, -10, 5, -5, 0])
    a = np.random.permutation(np.resize(levels, k // 512 * 4)).reshape(k // 512, 4)
    idx = np.arange(k)
    return np.exp2(a[idx // 512, idx % 128 // 32])


BF16 = ml_dtypes.bfloat16


def bf(x):
    return np.asarray(x, np.float32).astype(BF16)


def f64(x):
    return np.asarray(x).astype(np.float64)


NB, D1, KB, P, Q, LB, S = 2, 32, 8, 512, 512, 8, 64
D2 = KB * P
R = KB * Q // LB
DO = S * LB


def _blockdiag_butterfly_multiply(x, w1, w2):
    B, n = x.shape
    k, q, p = w1.shape
    l, s, r = w2.shape
    x_r = x.reshape(B, k, p).transpose(1, 0, 2)
    out1 = mxq(x_r, 2, "e4m3") @ mxq(w1, 2, "e4m3").transpose(0, 2, 1)
    out1 = out1.transpose(1, 0, 2).reshape(B, r, l).transpose(2, 0, 1)
    out2 = mxq(out1, 2, "e4m3") @ mxq(w2, 2, "e4m3").transpose(0, 2, 1)
    return out2.transpose(1, 2, 0).reshape(B, s * l)


def setup_inputs():
    s = mx_kscale(P)
    t = mx_kscale(R)
    tf = np.repeat(t, LB).reshape(KB, Q)
    return {"x": bf(np.random.standard_normal((NB, D1, D2)) * np.tile(s, KB)),
            "factorL": bf(np.random.standard_normal((KB, Q, P)) / np.sqrt(P) / s * tf[:, :, None]),
            "factorR": bf(np.random.standard_normal((LB, S, R)) / np.sqrt(R) / t),
            "bias": bf(np.random.standard_normal(DO) * 0.5)}


def reference(x, factorL, factorR, bias):
    b, d1, d2 = x.shape
    out = _blockdiag_butterfly_multiply(f64(x).reshape(-1, d2), f64(factorL), f64(factorR))
    out = out.reshape(b, d1, -1)
    return out + f64(bias)

@@ -1,0 +1,203 @@
+from contextlib import ExitStack
+
+import concourse.mybir as mybir
+from concourse.masks import make_identity
+
+FP8X4 = mybir.dt.float8_e4m3fn_x4
+BF16 = mybir.dt.bfloat16
+F32 = mybir.dt.float32
+I32 = mybir.dt.int32
+U32 = mybir.dt.uint32
+U8 = mybir.dt.uint8
+
+P = 128
+HALF = P // 2
+PACK = 4
+ROWS = 64
+K_PASS = 512
+BLOCKS = 8
+GROUPS = 8
+S_OUT = 64
+BLOCK_PAIRS = BLOCKS // 2
+GROUP_PAIRS = GROUPS // 2
+WORDS = K_PASS // 2
+CHUNK = 2 * K_PASS
+
+FLOPS = 2 * ROWS * BLOCKS * K_PASS * K_PASS + 2 * ROWS * GROUPS * K_PASS * S_OUT
+
+
+def tile_butterflyblocksparselinear_s_kernel(tc, x, factorL, factorR, bias, out):
+    nc = tc.nc
+    with ExitStack() as ctx:
+        keep = ctx.enter_context(tc.tile_pool(name="keep", bufs=1))
+        raw_pool = ctx.enter_context(tc.tile_pool(name="raw", bufs=GROUP_PAIRS * BLOCK_PAIRS))
+        stage = ctx.enter_context(tc.tile_pool(name="stage", bufs=4))
+        code_pool = ctx.enter_context(tc.tile_pool(name="codes", bufs=2 * BLOCK_PAIRS))
+        flip_pool = ctx.enter_context(tc.psum_pool(name="flip", bufs=5))
+        h_pool = ctx.enter_context(tc.psum_pool(name="h", bufs=2))
+        y_pool = ctx.enter_context(tc.psum_pool(name="y", bufs=1))
+        ctx.enter_context(tc.manual_schedule())
+
+        ident_f32 = keep.tile([P, P], F32)
+        make_identity(nc, ident_f32[:])
+        ident_bf16 = keep.tile([P, P], BF16)
+        make_identity(nc, ident_bf16[:])
+        ones = keep.tile([P, P], BF16)
+        nc.vector.memset(ones[:], 1.0)
+        bias_row = keep.tile([P, GROUPS * S_OUT], BF16)
+        nc.vector.memset(bias_row[:], 0.0)
+        g_codes = keep.tile([P, GROUPS * P], U32, align_bytes=64)
+        nc.vector.memset(g_codes[:].bitcast(I32), 0)
+        g_scales = keep.tile([P, GROUPS * P], U8, align_bytes=64)
+        nc.vector.memset(g_scales[:].bitcast(I32), 0)
+
+        r_raw = keep.tile([P, GROUP_PAIRS, K_PASS], BF16)
+        nc.sync.dma_start(out=r_raw[:], in_=factorR.rearrange("(lp l2) s r -> (l2 s) lp r", l2=2))
+        x_raw = keep.tile([P, BLOCKS // 2 * K_PASS], BF16)
+        nc.sync.dma_start(out=x_raw[:], in_=x.rearrange("a b (h c) -> (a b h) c", h=2))
+        nc.sync.dma_start(out=bias_row[0:1, :], in_=bias.rearrange("(o n) -> o n", o=1))
+        l_rows = factorL.rearrange("k (j l) p -> (k j) (l p)", l=GROUPS)
+        l_raw = {}
+        for lp in range(GROUP_PAIRS):
+            for kp in range(BLOCK_PAIRS):
+                chunk = raw_pool.tile([P, CHUNK], BF16)
+                nc.sync.dma_start(
+                    out=chunk[:],
+                    in_=l_rows[kp * P : (kp + 1) * P, lp * CHUNK : (lp + 1) * CHUNK],
+                )
+                l_raw[(lp, kp)] = chunk
+
+        r_grouped = keep.tile([P, GROUP_PAIRS, P, PACK], BF16, align_bytes=64)
+        for lp in range(GROUP_PAIRS):
+            r_flip = flip_pool.tile([P, PACK, P], BF16, tag="flip")
+            for t in range(PACK):
+                nc.tensor.transpose(r_flip[:, t, :], r_raw[:, lp, t * P : (t + 1) * P], ident_bf16[:])
+            nc.vector.tensor_copy(out=r_grouped[:, lp, :, :], in_=r_flip[:].rearrange("p t c -> p c t"))
+
+        x_words = x_raw[:].bitcast(F32)
+        x_grouped = keep.tile([P, BLOCKS * ROWS * PACK], BF16, align_bytes=64)
+        x_grouped_words = x_grouped[:].bitcast(F32).rearrange(
+            "p (kp k2 b u) -> p kp k2 b u", kp=BLOCK_PAIRS, k2=2, u=2
+        )
+        for i in range(2):
+            x_flip = flip_pool.tile([P, 2, 2, P], F32, tag="flip")
+            for k2 in range(2):
+                for u in range(2):
+                    first = (2 * i + k2) * WORDS + u * P
+                    nc.tensor.transpose(x_flip[:, k2, u, :], x_words[:, first : first + P], ident_f32[:])
+            by_half = x_flip[:].rearrange("p k2 u (b h) -> p h k2 b u", h=2)
+            copy_out = nc.vector.tensor_copy if i == 0 else nc.scalar.copy
+            for h in range(2):
+                copy_out(out=x_grouped_words[:, 2 * h + i, :, :, :], in_=by_half[:, h, :, :, :])
+
+        r_codes = keep.tile([P, GROUPS * S_OUT], U32, align_bytes=64)
+        r_scales = keep.tile([P, GROUPS * S_OUT], U8, align_bytes=64)
+        nc.vector.quantize_mx(
+            out=r_codes[:].bitcast(FP8X4),
+            scales=r_scales[:],
+            in_=r_grouped[:].rearrange("p lp c t -> p (lp c t)"),
+        )
+        x_codes = keep.tile([P, BLOCKS * ROWS], U32, align_bytes=64)
+        x_scales = keep.tile([P, BLOCKS * ROWS], U8, align_bytes=64)
+        nc.vector.quantize_mx(out=x_codes[:].bitcast(FP8X4), scales=x_scales[:], in_=x_grouped[:])
+
+        bias_flip = flip_pool.tile([P, GROUPS * S_OUT], F32, tag="flip")
+        nc.tensor.matmul(out=bias_flip[:], lhsT=ones[:], rhs=bias_row[:], start=True, stop=True)
+        bias_all = keep.tile([P, GROUPS * S_OUT], F32)
+        nc.scalar.copy(out=bias_all[:], in_=bias_flip[:])
+
+        l_quantised = {}
+        hidden = {}
+        y = y_pool.tile([P, GROUPS, S_OUT], F32)
+
+        def transpose_and_quantise(lp, kp):
+            raw_words = l_raw[(lp, kp)][:].bitcast(F32)
+            l_flip = flip_pool.tile([P, 2, 2, P], F32, tag="flip")
+            for l2 in range(2):
+                for u in range(2):
+                    first = l2 * WORDS + u * P
+                    nc.tensor.transpose(l_flip[:, l2, u, :], raw_words[:, first : first + P], ident_f32[:])
+            l_grouped = stage.tile([P, CHUNK], BF16, align_bytes=64)
+            nc.scalar.copy(
+                out=l_grouped[:].bitcast(F32).rearrange("p (l2 c u) -> p l2 c u", l2=2, u=2),
+                in_=l_flip[:].rearrange("p l2 u c -> p l2 c u"),
+            )
+            l_codes = code_pool.tile([P, 2 * P], U32, align_bytes=64)
+            l_scales = code_pool.tile([P, 2 * P], U8, align_bytes=64)
+            nc.vector.quantize_mx(out=l_codes[:].bitcast(FP8X4), scales=l_scales[:], in_=l_grouped[:])
+            l_quantised[(lp, kp)] = (l_codes, l_scales)
+
+        def first_product(lp):
+            for l2 in range(2):
+                hidden[l2] = h_pool.tile([P, BLOCK_PAIRS, P], F32, tag="h", name="hidden%d" % l2)
+            for kp in range(BLOCK_PAIRS):
+                l_codes, l_scales = l_quantised[(lp, kp)]
+                for l2 in range(2):
+                    nc.tensor.matmul_mx(
+                        out=hidden[l2][:, kp, :],
+                        lhsT=l_codes[:, l2 * P : (l2 + 1) * P].bitcast(FP8X4),
+                        lhsT_scale=l_scales[:, l2 * P : (l2 + 1) * P],
+                        rhs=x_codes[:, kp * P : (kp + 1) * P].bitcast(FP8X4),
+                        rhs_scale=x_scales[:, kp * P : (kp + 1) * P],
+                        start=True,
+                        stop=True,
+                    )
+
+        def quantise_hidden(lp):
+            g_grouped = {}
+            for l2 in range(2):
+                g_grouped[l2] = stage.tile([P, ROWS, PACK], BF16, align_bytes=64, tag="g", name="g%d" % l2)
+                for k2, copy_out in ((0, nc.vector.tensor_copy), (1, nc.scalar.copy)):
+                    half = slice(k2 * HALF, (k2 + 1) * HALF)
+                    own_rows = slice(k2 * ROWS, (k2 + 1) * ROWS)
+                    copy_out(
+                        out=g_grouped[l2][half, :, :],
+                        in_=hidden[l2][half, :, own_rows].rearrange("p t b -> p b t"),
+                    )
+            for l2 in range(2):
+                first = (2 * lp + l2) * P
+                nc.vector.quantize_mx(
+                    out=g_codes[:, first : first + ROWS].bitcast(FP8X4),
+                    scales=g_scales[:, first : first + ROWS],
+                    in_=g_grouped[l2][:].rearrange("p b t -> p (b t)"),
+                )
+
+        def second_product(lp):
+            for l in (2 * lp, 2 * lp + 1):
+                nc.tensor.matmul_mx(
+                    out=y[:, l, :],
+                    lhsT=g_codes[:, l * P : (l + 1) * P].bitcast(FP8X4),
+                    lhsT_scale=g_scales[:, l * P : (l + 1) * P],
+                    rhs=r_codes[:, l * S_OUT : (l + 1) * S_OUT].bitcast(FP8X4),
+                    rhs_scale=r_scales[:, l * S_OUT : (l + 1) * S_OUT],
+                    start=True,
+                    stop=True,
+                )
+
+        for lp in range(GROUP_PAIRS):
+            transpose_and_quantise(lp, 0)
+            if lp >= 2:
+                second_product(lp - 2)
+            if lp >= 1:
+                first_product(lp - 1)
+            transpose_and_quantise(lp, 1)
+            if lp >= 1:
+                quantise_hidden(lp - 1)
+            transpose_and_quantise(lp, 2)
+            transpose_and_quantise(lp, 3)
+        second_product(GROUP_PAIRS - 2)
+        first_product(GROUP_PAIRS - 1)
+        quantise_hidden(GROUP_PAIRS - 1)
+        second_product(GROUP_PAIRS - 1)
+
+        out_rows = keep.tile([ROWS, S_OUT, GROUPS], F32)
+        nc.vector.tensor_tensor(
+            out=out_rows[:],
+            in0=y[0:ROWS, :, :].rearrange("b l s -> b s l"),
+            in1=bias_all[0:ROWS, :].rearrange("b (s l) -> b s l", l=GROUPS),
+            op=mybir.AluOpType.add,
+        )
+        nc.sync.dma_start(
+            out=out.rearrange("a b n -> (a b) n"),
+            in_=out_rows[:].rearrange("b s l -> b (s l)"),
+        )

@@ -31,8 +31,8 @@ def tile_butterflyblocksparselinear_s_kernel(tc, x, factorL, factorR, bias, out)
     with ExitStack() as ctx:
         keep = ctx.enter_context(tc.tile_pool(name="keep", bufs=1))
         raw_pool = ctx.enter_context(tc.tile_pool(name="raw", bufs=GROUP_PAIRS * BLOCK_PAIRS))
-        stage = ctx.enter_context(tc.tile_pool(name="stage", bufs=4))
-        code_pool = ctx.enter_context(tc.tile_pool(name="codes", bufs=2 * BLOCK_PAIRS))
+        stage = ctx.enter_context(tc.tile_pool(name="stage", bufs=2 * BLOCK_PAIRS))
+        code_pool = ctx.enter_context(tc.tile_pool(name="codes", bufs=GROUP_PAIRS * BLOCK_PAIRS))
         flip_pool = ctx.enter_context(tc.psum_pool(name="flip", bufs=5))
         h_pool = ctx.enter_context(tc.psum_pool(name="h", bufs=2))
         y_pool = ctx.enter_context(tc.psum_pool(name="y", bufs=1))
@@ -42,23 +42,15 @@ def tile_butterflyblocksparselinear_s_kernel(tc, x, factorL, factorR, bias, out)
         make_identity(nc, ident_f32[:])
         ident_bf16 = keep.tile([P, P], BF16)
         make_identity(nc, ident_bf16[:])
-        ones = keep.tile([P, P], BF16)
-        nc.vector.memset(ones[:], 1.0)
-        bias_row = keep.tile([P, GROUPS * S_OUT], BF16)
-        nc.vector.memset(bias_row[:], 0.0)
         g_codes = keep.tile([P, GROUPS * P], U32, align_bytes=64)
         nc.vector.memset(g_codes[:].bitcast(I32), 0)
         g_scales = keep.tile([P, GROUPS * P], U8, align_bytes=64)
         nc.vector.memset(g_scales[:].bitcast(I32), 0)
 
-        r_raw = keep.tile([P, GROUP_PAIRS, K_PASS], BF16)
-        nc.sync.dma_start(out=r_raw[:], in_=factorR.rearrange("(lp l2) s r -> (l2 s) lp r", l2=2))
-        x_raw = keep.tile([P, BLOCKS // 2 * K_PASS], BF16)
-        nc.sync.dma_start(out=x_raw[:], in_=x.rearrange("a b (h c) -> (a b h) c", h=2))
-        nc.sync.dma_start(out=bias_row[0:1, :], in_=bias.rearrange("(o n) -> o n", o=1))
         l_rows = factorL.rearrange("k (j l) p -> (k j) (l p)", l=GROUPS)
         l_raw = {}
-        for lp in range(GROUP_PAIRS):
+
+        def load_group_pair(lp):
             for kp in range(BLOCK_PAIRS):
                 chunk = raw_pool.tile([P, CHUNK], BF16)
                 nc.sync.dma_start(
@@ -67,44 +59,53 @@ def tile_butterflyblocksparselinear_s_kernel(tc, x, factorL, factorR, bias, out)
                 )
                 l_raw[(lp, kp)] = chunk
 
-        r_grouped = keep.tile([P, GROUP_PAIRS, P, PACK], BF16, align_bytes=64)
-        for lp in range(GROUP_PAIRS):
-            r_flip = flip_pool.tile([P, PACK, P], BF16, tag="flip")
-            for t in range(PACK):
-                nc.tensor.transpose(r_flip[:, t, :], r_raw[:, lp, t * P : (t + 1) * P], ident_bf16[:])
-            nc.vector.tensor_copy(out=r_grouped[:, lp, :, :], in_=r_flip[:].rearrange("p t c -> p c t"))
+        load_group_pair(0)
+        x_raw = keep.tile([P, BLOCKS // 2 * K_PASS], BF16)
+        nc.sync.dma_start(out=x_raw[:], in_=x.rearrange("a b (h c) -> (a b h) c", h=2))
+        load_group_pair(1)
+        r_raw = keep.tile([P, GROUP_PAIRS, K_PASS], BF16)
+        nc.sync.dma_start(out=r_raw[:], in_=factorR.rearrange("(lp l2) s r -> (l2 s) lp r", l2=2))
+        load_group_pair(2)
+        load_group_pair(3)
+        bias_rows = keep.tile([ROWS, GROUPS * S_OUT], BF16)
+        nc.sync.dma_start(out=bias_rows[:], in_=bias.partition_broadcast(ROWS))
 
-        x_words = x_raw[:].bitcast(F32)
-        x_grouped = keep.tile([P, BLOCKS * ROWS * PACK], BF16, align_bytes=64)
-        x_grouped_words = x_grouped[:].bitcast(F32).rearrange(
-            "p (kp k2 b u) -> p kp k2 b u", kp=BLOCK_PAIRS, k2=2, u=2
-        )
-        for i in range(2):
-            x_flip = flip_pool.tile([P, 2, 2, P], F32, tag="flip")
-            for k2 in range(2):
-                for u in range(2):
-                    first = (2 * i + k2) * WORDS + u * P
-                    nc.tensor.transpose(x_flip[:, k2, u, :], x_words[:, first : first + P], ident_f32[:])
-            by_half = x_flip[:].rearrange("p k2 u (b h) -> p h k2 b u", h=2)
-            copy_out = nc.vector.tensor_copy if i == 0 else nc.scalar.copy
-            for h in range(2):
-                copy_out(out=x_grouped_words[:, 2 * h + i, :, :, :], in_=by_half[:, h, :, :, :])
+        x_codes = keep.tile([P, BLOCKS * ROWS], U32, align_bytes=64)
+        x_scales = keep.tile([P, BLOCKS * ROWS], U8, align_bytes=64)
+
+        def prepare_x():
+            x_words = x_raw[:].bitcast(F32)
+            x_grouped = keep.tile([P, BLOCKS * ROWS * PACK], BF16, align_bytes=64)
+            x_grouped_words = x_grouped[:].bitcast(F32).rearrange(
+                "p (kp k2 b u) -> p kp k2 b u", kp=BLOCK_PAIRS, k2=2, u=2
+            )
+            for i in range(2):
+                x_flip = flip_pool.tile([P, 2, 2, P], F32, tag="flip")
+                for k2 in range(2):
+                    for u in range(2):
+                        first = (2 * i + k2) * WORDS + u * P
+                        nc.tensor.transpose(x_flip[:, k2, u, :], x_words[:, first : first + P], ident_f32[:])
+                by_half = x_flip[:].rearrange("p k2 u (b h) -> p h k2 b u", h=2)
+                copy_out = nc.vector.tensor_copy if i == 0 else nc.scalar.copy
+                for h in range(2):
+                    copy_out(out=x_grouped_words[:, 2 * h + i, :, :, :], in_=by_half[:, h, :, :, :])
+            nc.vector.quantize_mx(out=x_codes[:].bitcast(FP8X4), scales=x_scales[:], in_=x_grouped[:])
 
         r_codes = keep.tile([P, GROUPS * S_OUT], U32, align_bytes=64)
         r_scales = keep.tile([P, GROUPS * S_OUT], U8, align_bytes=64)
-        nc.vector.quantize_mx(
-            out=r_codes[:].bitcast(FP8X4),
-            scales=r_scales[:],
-            in_=r_grouped[:].rearrange("p lp c t -> p (lp c t)"),
-        )
-        x_codes = keep.tile([P, BLOCKS * ROWS], U32, align_bytes=64)
-        x_scales = keep.tile([P, BLOCKS * ROWS], U8, align_bytes=64)
-        nc.vector.quantize_mx(out=x_codes[:].bitcast(FP8X4), scales=x_scales[:], in_=x_grouped[:])
 
-        bias_flip = flip_pool.tile([P, GROUPS * S_OUT], F32, tag="flip")
-        nc.tensor.matmul(out=bias_flip[:], lhsT=ones[:], rhs=bias_row[:], start=True, stop=True)
-        bias_all = keep.tile([P, GROUPS * S_OUT], F32)
-        nc.scalar.copy(out=bias_all[:], in_=bias_flip[:])
+        def prepare_factor_r():
+            r_grouped = keep.tile([P, GROUP_PAIRS, P, PACK], BF16, align_bytes=64)
+            for lp in range(GROUP_PAIRS):
+                r_flip = flip_pool.tile([P, PACK, P], BF16, tag="flip")
+                for t in range(PACK):
+                    nc.tensor.transpose(r_flip[:, t, :], r_raw[:, lp, t * P : (t + 1) * P], ident_bf16[:])
+                nc.vector.tensor_copy(out=r_grouped[:, lp, :, :], in_=r_flip[:].rearrange("p t c -> p c t"))
+            nc.vector.quantize_mx(
+                out=r_codes[:].bitcast(FP8X4),
+                scales=r_scales[:],
+                in_=r_grouped[:].rearrange("p lp c t -> p (lp c t)"),
+            )
 
         l_quantised = {}
         hidden = {}
@@ -175,18 +176,20 @@ def tile_butterflyblocksparselinear_s_kernel(tc, x, factorL, factorR, bias, out)
                 )
 
         for lp in range(GROUP_PAIRS):
-            transpose_and_quantise(lp, 0)
+            for kp in range(BLOCK_PAIRS):
+                transpose_and_quantise(lp, kp)
+            if lp == 0:
+                prepare_x()
+            if lp >= 1:
+                first_product(lp - 1)
             if lp >= 2:
                 second_product(lp - 2)
             if lp >= 1:
-                first_product(lp - 1)
-            transpose_and_quantise(lp, 1)
-            if lp >= 1:
                 quantise_hidden(lp - 1)
-            transpose_and_quantise(lp, 2)
-            transpose_and_quantise(lp, 3)
-        second_product(GROUP_PAIRS - 2)
+            if lp == 1:
+                prepare_factor_r()
         first_product(GROUP_PAIRS - 1)
+        second_product(GROUP_PAIRS - 2)
         quantise_hidden(GROUP_PAIRS - 1)
         second_product(GROUP_PAIRS - 1)
 
@@ -194,7 +197,7 @@ def tile_butterflyblocksparselinear_s_kernel(tc, x, factorL, factorR, bias, out)
         nc.vector.tensor_tensor(
             out=out_rows[:],
             in0=y[0:ROWS, :, :].rearrange("b l s -> b s l"),
-            in1=bias_all[0:ROWS, :].rearrange("b (s l) -> b s l", l=GROUPS),
+            in1=bias_rows[:].rearrange("b (s l) -> b s l", l=GROUPS),
             op=mybir.AluOpType.add,
         )
         nc.sync.dma_start(

@@ -22,6 +22,11 @@ BLOCK_PAIRS = BLOCKS // 2
 GROUP_PAIRS = GROUPS // 2
 WORDS = K_PASS // 2
 CHUNK = 2 * K_PASS
+CHUNKS = BLOCK_PAIRS // 2
+
+FIRST_LAG = 2
+SECOND_LAG = 5
+HEAD_WARM = 4
 
 FLOPS = 2 * ROWS * BLOCKS * K_PASS * K_PASS + 2 * ROWS * GROUPS * K_PASS * S_OUT
 
@@ -30,43 +35,64 @@ def tile_butterflyblocksparselinear_s_kernel(tc, x, factorL, factorR, bias, out)
     nc = tc.nc
     with ExitStack() as ctx:
         keep = ctx.enter_context(tc.tile_pool(name="keep", bufs=1))
-        raw_pool = ctx.enter_context(tc.tile_pool(name="raw", bufs=GROUP_PAIRS * BLOCK_PAIRS))
-        stage = ctx.enter_context(tc.tile_pool(name="stage", bufs=2 * BLOCK_PAIRS))
-        code_pool = ctx.enter_context(tc.tile_pool(name="codes", bufs=GROUP_PAIRS * BLOCK_PAIRS))
-        flip_pool = ctx.enter_context(tc.psum_pool(name="flip", bufs=5))
+        raw_pool = ctx.enter_context(tc.tile_pool(name="raw", bufs=GROUPS * CHUNKS))
+        code_pool = ctx.enter_context(tc.tile_pool(name="codes", bufs=GROUPS * CHUNKS))
+        stage = ctx.enter_context(tc.tile_pool(name="stage", bufs=8))
+        flip_pool = ctx.enter_context(tc.psum_pool(name="flip", bufs=4))
         h_pool = ctx.enter_context(tc.psum_pool(name="h", bufs=2))
         y_pool = ctx.enter_context(tc.psum_pool(name="y", bufs=1))
+        idle_pool = ctx.enter_context(tc.psum_pool(name="idle", bufs=1))
         ctx.enter_context(tc.manual_schedule())
 
-        ident_f32 = keep.tile([P, P], F32)
-        make_identity(nc, ident_f32[:])
-        ident_bf16 = keep.tile([P, P], BF16)
-        make_identity(nc, ident_bf16[:])
+        zeros = keep.tile([P, K_PASS * PACK], BF16, align_bytes=64)
+        nc.vector.memset(zeros[:].bitcast(I32), 0)
+        zero_codes = keep.tile([P, K_PASS], U32, align_bytes=64)
+        zero_scales = keep.tile([P, K_PASS], U8, align_bytes=64)
+        nc.vector.quantize_mx(out=zero_codes[:].bitcast(FP8X4), scales=zero_scales[:], in_=zeros[:])
         g_codes = keep.tile([P, GROUPS * P], U32, align_bytes=64)
         nc.vector.memset(g_codes[:].bitcast(I32), 0)
         g_scales = keep.tile([P, GROUPS * P], U8, align_bytes=64)
         nc.vector.memset(g_scales[:].bitcast(I32), 0)
+        ident_f32 = keep.tile([P, P], F32)
+        make_identity(nc, ident_f32[:])
+        ident_bf16 = keep.tile([P, P], BF16)
+        make_identity(nc, ident_bf16[:])
+
+        idle_bank = idle_pool.tile([P, K_PASS], F32)
+
+        def keep_clock_up():
+            nc.tensor.matmul_mx(
+                out=idle_bank[:],
+                lhsT=zero_codes[:, 0:P].bitcast(FP8X4),
+                lhsT_scale=zero_scales[:, 0:P],
+                rhs=zero_codes[:].bitcast(FP8X4),
+                rhs_scale=zero_scales[:],
+                start=True,
+                stop=True,
+            )
 
         l_rows = factorL.rearrange("k (j l) p -> (k j) (l p)", l=GROUPS)
         l_raw = {}
 
-        def load_group_pair(lp):
-            for kp in range(BLOCK_PAIRS):
+        def load_group(l):
+            for a in range(CHUNKS):
                 chunk = raw_pool.tile([P, CHUNK], BF16)
                 nc.sync.dma_start(
-                    out=chunk[:],
-                    in_=l_rows[kp * P : (kp + 1) * P, lp * CHUNK : (lp + 1) * CHUNK],
+                    out=chunk[:].rearrange("w (kp2 p) -> w kp2 p", kp2=2),
+                    in_=l_rows[a * 2 * P : (a + 1) * 2 * P, l * K_PASS : (l + 1) * K_PASS].rearrange(
+                        "(kp2 w) p -> w kp2 p", kp2=2
+                    ),
                 )
-                l_raw[(lp, kp)] = chunk
+                l_raw[(l, a)] = chunk
 
-        load_group_pair(0)
         x_raw = keep.tile([P, BLOCKS // 2 * K_PASS], BF16)
         nc.sync.dma_start(out=x_raw[:], in_=x.rearrange("a b (h c) -> (a b h) c", h=2))
-        load_group_pair(1)
+        load_group(0)
+        load_group(1)
         r_raw = keep.tile([P, GROUP_PAIRS, K_PASS], BF16)
         nc.sync.dma_start(out=r_raw[:], in_=factorR.rearrange("(lp l2) s r -> (l2 s) lp r", l2=2))
-        load_group_pair(2)
-        load_group_pair(3)
+        for l in range(2, GROUPS):
+            load_group(l)
         bias_rows = keep.tile([ROWS, GROUPS * S_OUT], BF16)
         nc.sync.dma_start(out=bias_rows[:], in_=bias.partition_broadcast(ROWS))
 
@@ -111,87 +137,83 @@ def tile_butterflyblocksparselinear_s_kernel(tc, x, factorL, factorR, bias, out)
         hidden = {}
         y = y_pool.tile([P, GROUPS, S_OUT], F32)
 
-        def transpose_and_quantise(lp, kp):
-            raw_words = l_raw[(lp, kp)][:].bitcast(F32)
-            l_flip = flip_pool.tile([P, 2, 2, P], F32, tag="flip")
-            for l2 in range(2):
-                for u in range(2):
-                    first = l2 * WORDS + u * P
-                    nc.tensor.transpose(l_flip[:, l2, u, :], raw_words[:, first : first + P], ident_f32[:])
-            l_grouped = stage.tile([P, CHUNK], BF16, align_bytes=64)
-            nc.scalar.copy(
-                out=l_grouped[:].bitcast(F32).rearrange("p (l2 c u) -> p l2 c u", l2=2, u=2),
-                in_=l_flip[:].rearrange("p l2 u c -> p l2 c u"),
-            )
-            l_codes = code_pool.tile([P, 2 * P], U32, align_bytes=64)
-            l_scales = code_pool.tile([P, 2 * P], U8, align_bytes=64)
-            nc.vector.quantize_mx(out=l_codes[:].bitcast(FP8X4), scales=l_scales[:], in_=l_grouped[:])
-            l_quantised[(lp, kp)] = (l_codes, l_scales)
-
-        def first_product(lp):
-            for l2 in range(2):
-                hidden[l2] = h_pool.tile([P, BLOCK_PAIRS, P], F32, tag="h", name="hidden%d" % l2)
-            for kp in range(BLOCK_PAIRS):
-                l_codes, l_scales = l_quantised[(lp, kp)]
-                for l2 in range(2):
-                    nc.tensor.matmul_mx(
-                        out=hidden[l2][:, kp, :],
-                        lhsT=l_codes[:, l2 * P : (l2 + 1) * P].bitcast(FP8X4),
-                        lhsT_scale=l_scales[:, l2 * P : (l2 + 1) * P],
-                        rhs=x_codes[:, kp * P : (kp + 1) * P].bitcast(FP8X4),
-                        rhs_scale=x_scales[:, kp * P : (kp + 1) * P],
-                        start=True,
-                        stop=True,
-                    )
-
-        def quantise_hidden(lp):
-            g_grouped = {}
-            for l2 in range(2):
-                g_grouped[l2] = stage.tile([P, ROWS, PACK], BF16, align_bytes=64, tag="g", name="g%d" % l2)
-                for k2, copy_out in ((0, nc.vector.tensor_copy), (1, nc.scalar.copy)):
-                    half = slice(k2 * HALF, (k2 + 1) * HALF)
-                    own_rows = slice(k2 * ROWS, (k2 + 1) * ROWS)
-                    copy_out(
-                        out=g_grouped[l2][half, :, :],
-                        in_=hidden[l2][half, :, own_rows].rearrange("p t b -> p b t"),
-                    )
-            for l2 in range(2):
-                first = (2 * lp + l2) * P
-                nc.vector.quantize_mx(
-                    out=g_codes[:, first : first + ROWS].bitcast(FP8X4),
-                    scales=g_scales[:, first : first + ROWS],
-                    in_=g_grouped[l2][:].rearrange("p b t -> p (b t)"),
+        def transpose_and_quantise(l):
+            for a in range(CHUNKS):
+                raw_words = l_raw[(l, a)][:].bitcast(F32)
+                l_flip = flip_pool.tile([P, 2, 2, P], F32, tag="flip")
+                for kp2 in range(2):
+                    for u in range(2):
+                        first = kp2 * WORDS + u * P
+                        nc.tensor.transpose(l_flip[:, kp2, u, :], raw_words[:, first : first + P], ident_f32[:])
+                l_grouped = stage.tile([P, CHUNK], BF16, align_bytes=64)
+                nc.scalar.copy(
+                    out=l_grouped[:].bitcast(F32).rearrange("p (kp2 c u) -> p kp2 c u", kp2=2, u=2),
+                    in_=l_flip[:].rearrange("p kp2 u c -> p kp2 c u"),
                 )
+                l_codes = code_pool.tile([P, 2 * P], U32, align_bytes=64)
+                l_scales = code_pool.tile([P, 2 * P], U8, align_bytes=64)
+                nc.vector.quantize_mx(out=l_codes[:].bitcast(FP8X4), scales=l_scales[:], in_=l_grouped[:])
+                l_quantised[(l, a)] = (l_codes, l_scales)
 
-        def second_product(lp):
-            for l in (2 * lp, 2 * lp + 1):
+        def first_product(l):
+            h_bank = h_pool.tile([P, BLOCK_PAIRS, P], F32)
+            hidden[l] = h_bank
+            for kp in range(BLOCK_PAIRS):
+                l_codes, l_scales = l_quantised[(l, kp // 2)]
+                cols = slice(kp % 2 * P, (kp % 2 + 1) * P)
                 nc.tensor.matmul_mx(
-                    out=y[:, l, :],
-                    lhsT=g_codes[:, l * P : (l + 1) * P].bitcast(FP8X4),
-                    lhsT_scale=g_scales[:, l * P : (l + 1) * P],
-                    rhs=r_codes[:, l * S_OUT : (l + 1) * S_OUT].bitcast(FP8X4),
-                    rhs_scale=r_scales[:, l * S_OUT : (l + 1) * S_OUT],
+                    out=h_bank[:, kp, :],
+                    lhsT=l_codes[:, cols].bitcast(FP8X4),
+                    lhsT_scale=l_scales[:, cols],
+                    rhs=x_codes[:, kp * P : (kp + 1) * P].bitcast(FP8X4),
+                    rhs_scale=x_scales[:, kp * P : (kp + 1) * P],
                     start=True,
                     stop=True,
                 )
 
-        for lp in range(GROUP_PAIRS):
-            for kp in range(BLOCK_PAIRS):
-                transpose_and_quantise(lp, kp)
-            if lp == 0:
-                prepare_x()
-            if lp >= 1:
-                first_product(lp - 1)
-            if lp >= 2:
-                second_product(lp - 2)
-            if lp >= 1:
-                quantise_hidden(lp - 1)
-            if lp == 1:
+        def quantise_hidden(l):
+            g_grouped = stage.tile([P, ROWS, PACK], BF16, align_bytes=64)
+            for k2, copy_out in ((0, nc.vector.tensor_copy), (1, nc.scalar.copy)):
+                half = slice(k2 * HALF, (k2 + 1) * HALF)
+                own_rows = slice(k2 * ROWS, (k2 + 1) * ROWS)
+                copy_out(
+                    out=g_grouped[half, :, :],
+                    in_=hidden[l][half, :, own_rows].rearrange("p t b -> p b t"),
+                )
+            nc.vector.quantize_mx(
+                out=g_codes[:, l * P : l * P + ROWS].bitcast(FP8X4),
+                scales=g_scales[:, l * P : l * P + ROWS],
+                in_=g_grouped[:].rearrange("p b t -> p (b t)"),
+            )
+
+        def second_product(l):
+            nc.tensor.matmul_mx(
+                out=y[:, l, :],
+                lhsT=g_codes[:, l * P : (l + 1) * P].bitcast(FP8X4),
+                lhsT_scale=g_scales[:, l * P : (l + 1) * P],
+                rhs=r_codes[:, l * S_OUT : (l + 1) * S_OUT].bitcast(FP8X4),
+                rhs_scale=r_scales[:, l * S_OUT : (l + 1) * S_OUT],
+                start=True,
+                stop=True,
+            )
+
+        for i in range(HEAD_WARM):
+            keep_clock_up()
+        prepare_x()
+        keep_clock_up()
+        for step in range(GROUPS + SECOND_LAG):
+            if step < GROUPS:
+                transpose_and_quantise(step)
+            if step == 1:
                 prepare_factor_r()
-        first_product(GROUP_PAIRS - 1)
-        second_product(GROUP_PAIRS - 2)
-        quantise_hidden(GROUP_PAIRS - 1)
-        second_product(GROUP_PAIRS - 1)
+            if step < GROUPS:
+                keep_clock_up()
+            if 0 <= step - FIRST_LAG < GROUPS:
+                first_product(step - FIRST_LAG)
+            if 0 <= step - SECOND_LAG:
+                second_product(step - SECOND_LAG)
+            if 0 <= step - FIRST_LAG < GROUPS:
+                quantise_hidden(step - FIRST_LAG)
 
         out_rows = keep.tile([ROWS, S_OUT, GROUPS], F32)
         nc.vector.tensor_tensor(

@@ -21,12 +21,8 @@ S_OUT = 64
 BLOCK_PAIRS = BLOCKS // 2
 GROUP_PAIRS = GROUPS // 2
 WORDS = K_PASS // 2
+R_PIECES = GROUPS * S_OUT * PACK // P
 CHUNK = 2 * K_PASS
-CHUNKS = BLOCK_PAIRS // 2
-
-FIRST_LAG = 2
-SECOND_LAG = 5
-HEAD_WARM = 4
 
 FLOPS = 2 * ROWS * BLOCKS * K_PASS * K_PASS + 2 * ROWS * GROUPS * K_PASS * S_OUT
 
@@ -35,64 +31,45 @@ def tile_butterflyblocksparselinear_s_kernel(tc, x, factorL, factorR, bias, out)
     nc = tc.nc
     with ExitStack() as ctx:
         keep = ctx.enter_context(tc.tile_pool(name="keep", bufs=1))
-        raw_pool = ctx.enter_context(tc.tile_pool(name="raw", bufs=GROUPS * CHUNKS))
-        code_pool = ctx.enter_context(tc.tile_pool(name="codes", bufs=GROUPS * CHUNKS))
-        stage = ctx.enter_context(tc.tile_pool(name="stage", bufs=8))
-        flip_pool = ctx.enter_context(tc.psum_pool(name="flip", bufs=4))
+        raw_pool = ctx.enter_context(tc.tile_pool(name="raw", bufs=GROUP_PAIRS * BLOCK_PAIRS))
+        stage = ctx.enter_context(tc.tile_pool(name="stage", bufs=2 * BLOCK_PAIRS))
+        code_pool = ctx.enter_context(tc.tile_pool(name="codes", bufs=GROUP_PAIRS * BLOCK_PAIRS))
+        flip_pool = ctx.enter_context(tc.psum_pool(name="flip", bufs=5))
         h_pool = ctx.enter_context(tc.psum_pool(name="h", bufs=2))
         y_pool = ctx.enter_context(tc.psum_pool(name="y", bufs=1))
-        idle_pool = ctx.enter_context(tc.psum_pool(name="idle", bufs=1))
-        ctx.enter_context(tc.manual_schedule())
 
-        zeros = keep.tile([P, K_PASS * PACK], BF16, align_bytes=64)
-        nc.vector.memset(zeros[:].bitcast(I32), 0)
-        zero_codes = keep.tile([P, K_PASS], U32, align_bytes=64)
-        zero_scales = keep.tile([P, K_PASS], U8, align_bytes=64)
-        nc.vector.quantize_mx(out=zero_codes[:].bitcast(FP8X4), scales=zero_scales[:], in_=zeros[:])
-        g_codes = keep.tile([P, GROUPS * P], U32, align_bytes=64)
-        nc.vector.memset(g_codes[:].bitcast(I32), 0)
-        g_scales = keep.tile([P, GROUPS * P], U8, align_bytes=64)
-        nc.vector.memset(g_scales[:].bitcast(I32), 0)
         ident_f32 = keep.tile([P, P], F32)
         make_identity(nc, ident_f32[:])
         ident_bf16 = keep.tile([P, P], BF16)
         make_identity(nc, ident_bf16[:])
-
-        idle_bank = idle_pool.tile([P, K_PASS], F32)
-
-        def keep_clock_up():
-            nc.tensor.matmul_mx(
-                out=idle_bank[:],
-                lhsT=zero_codes[:, 0:P].bitcast(FP8X4),
-                lhsT_scale=zero_scales[:, 0:P],
-                rhs=zero_codes[:].bitcast(FP8X4),
-                rhs_scale=zero_scales[:],
-                start=True,
-                stop=True,
-            )
+        g_codes = keep.tile([P, GROUPS * P], U32, align_bytes=64)
+        nc.vector.memset(g_codes[:].bitcast(I32), 0)
+        g_scales = keep.tile([P, GROUPS * P], U8, align_bytes=64)
+        nc.vector.memset(g_scales[:].bitcast(I32), 0)
 
         l_rows = factorL.rearrange("k (j l) p -> (k j) (l p)", l=GROUPS)
         l_raw = {}
 
-        def load_group(l):
-            for a in range(CHUNKS):
+        def load_group_pair(lp):
+            for kp in range(BLOCK_PAIRS):
                 chunk = raw_pool.tile([P, CHUNK], BF16)
                 nc.sync.dma_start(
-                    out=chunk[:].rearrange("w (kp2 p) -> w kp2 p", kp2=2),
-                    in_=l_rows[a * 2 * P : (a + 1) * 2 * P, l * K_PASS : (l + 1) * K_PASS].rearrange(
-                        "(kp2 w) p -> w kp2 p", kp2=2
-                    ),
+                    out=chunk[:],
+                    in_=l_rows[kp * P : (kp + 1) * P, lp * CHUNK : (lp + 1) * CHUNK],
                 )
-                l_raw[(l, a)] = chunk
+                l_raw[(lp, kp)] = chunk
 
+        load_group_pair(0)
         x_raw = keep.tile([P, BLOCKS // 2 * K_PASS], BF16)
         nc.sync.dma_start(out=x_raw[:], in_=x.rearrange("a b (h c) -> (a b h) c", h=2))
-        load_group(0)
-        load_group(1)
-        r_raw = keep.tile([P, GROUP_PAIRS, K_PASS], BF16)
-        nc.sync.dma_start(out=r_raw[:], in_=factorR.rearrange("(lp l2) s r -> (l2 s) lp r", l2=2))
-        for l in range(2, GROUPS):
-            load_group(l)
+        load_group_pair(1)
+        load_group_pair(2)
+        load_group_pair(3)
+        r_raw = keep.tile([P, R_PIECES, P], BF16)
+        nc.sync.dma_start(
+            out=r_raw[:],
+            in_=factorR.rearrange("l s (t w) -> (l s t) w", t=PACK).rearrange("(n p) w -> p n w", p=P),
+        )
         bias_rows = keep.tile([ROWS, GROUPS * S_OUT], BF16)
         nc.sync.dma_start(out=bias_rows[:], in_=bias.partition_broadcast(ROWS))
 
@@ -121,99 +98,100 @@ def tile_butterflyblocksparselinear_s_kernel(tc, x, factorL, factorR, bias, out)
         r_scales = keep.tile([P, GROUPS * S_OUT], U8, align_bytes=64)
 
         def prepare_factor_r():
-            r_grouped = keep.tile([P, GROUP_PAIRS, P, PACK], BF16, align_bytes=64)
-            for lp in range(GROUP_PAIRS):
-                r_flip = flip_pool.tile([P, PACK, P], BF16, tag="flip")
-                for t in range(PACK):
-                    nc.tensor.transpose(r_flip[:, t, :], r_raw[:, lp, t * P : (t + 1) * P], ident_bf16[:])
-                nc.vector.tensor_copy(out=r_grouped[:, lp, :, :], in_=r_flip[:].rearrange("p t c -> p c t"))
-            nc.vector.quantize_mx(
-                out=r_codes[:].bitcast(FP8X4),
-                scales=r_scales[:],
-                in_=r_grouped[:].rearrange("p lp c t -> p (lp c t)"),
-            )
+            r_grouped = keep.tile([P, GROUPS * S_OUT * PACK], BF16, align_bytes=64)
+            per_bank = R_PIECES // 2
+            for i in range(2):
+                r_flip = flip_pool.tile([P, per_bank, P], BF16, tag="flip")
+                for n in range(per_bank):
+                    nc.tensor.transpose(r_flip[:, n, :], r_raw[:, i * per_bank + n, :], ident_bf16[:])
+                copy_out = nc.vector.tensor_copy if i == 0 else nc.scalar.copy
+                copy_out(
+                    out=r_grouped[:, i * per_bank * P : (i + 1) * per_bank * P],
+                    in_=r_flip[:].rearrange("p n c -> p (n c)"),
+                )
+            nc.vector.quantize_mx(out=r_codes[:].bitcast(FP8X4), scales=r_scales[:], in_=r_grouped[:])
 
         l_quantised = {}
         hidden = {}
         y = y_pool.tile([P, GROUPS, S_OUT], F32)
 
-        def transpose_and_quantise(l):
-            for a in range(CHUNKS):
-                raw_words = l_raw[(l, a)][:].bitcast(F32)
-                l_flip = flip_pool.tile([P, 2, 2, P], F32, tag="flip")
-                for kp2 in range(2):
-                    for u in range(2):
-                        first = kp2 * WORDS + u * P
-                        nc.tensor.transpose(l_flip[:, kp2, u, :], raw_words[:, first : first + P], ident_f32[:])
-                l_grouped = stage.tile([P, CHUNK], BF16, align_bytes=64)
-                nc.scalar.copy(
-                    out=l_grouped[:].bitcast(F32).rearrange("p (kp2 c u) -> p kp2 c u", kp2=2, u=2),
-                    in_=l_flip[:].rearrange("p kp2 u c -> p kp2 c u"),
-                )
-                l_codes = code_pool.tile([P, 2 * P], U32, align_bytes=64)
-                l_scales = code_pool.tile([P, 2 * P], U8, align_bytes=64)
-                nc.vector.quantize_mx(out=l_codes[:].bitcast(FP8X4), scales=l_scales[:], in_=l_grouped[:])
-                l_quantised[(l, a)] = (l_codes, l_scales)
+        def transpose_and_quantise(lp, kp):
+            raw_words = l_raw[(lp, kp)][:].bitcast(F32)
+            l_flip = flip_pool.tile([P, 2, 2, P], F32, tag="flip")
+            for l2 in range(2):
+                for u in range(2):
+                    first = l2 * WORDS + u * P
+                    nc.tensor.transpose(l_flip[:, l2, u, :], raw_words[:, first : first + P], ident_f32[:])
+            l_grouped = stage.tile([P, CHUNK], BF16, align_bytes=64)
+            nc.scalar.copy(
+                out=l_grouped[:].bitcast(F32).rearrange("p (l2 c u) -> p l2 c u", l2=2, u=2),
+                in_=l_flip[:].rearrange("p l2 u c -> p l2 c u"),
+            )
+            l_codes = code_pool.tile([P, 2 * P], U32, align_bytes=64)
+            l_scales = code_pool.tile([P, 2 * P], U8, align_bytes=64)
+            nc.vector.quantize_mx(out=l_codes[:].bitcast(FP8X4), scales=l_scales[:], in_=l_grouped[:])
+            l_quantised[(lp, kp)] = (l_codes, l_scales)
 
-        def first_product(l):
-            h_bank = h_pool.tile([P, BLOCK_PAIRS, P], F32)
-            hidden[l] = h_bank
+        def first_product(lp):
+            for l2 in range(2):
+                hidden[l2] = h_pool.tile([P, BLOCK_PAIRS, P], F32, tag="h", name="hidden%d" % l2)
             for kp in range(BLOCK_PAIRS):
-                l_codes, l_scales = l_quantised[(l, kp // 2)]
-                cols = slice(kp % 2 * P, (kp % 2 + 1) * P)
+                l_codes, l_scales = l_quantised[(lp, kp)]
+                for l2 in range(2):
+                    nc.tensor.matmul_mx(
+                        out=hidden[l2][:, kp, :],
+                        lhsT=l_codes[:, l2 * P : (l2 + 1) * P].bitcast(FP8X4),
+                        lhsT_scale=l_scales[:, l2 * P : (l2 + 1) * P],
+                        rhs=x_codes[:, kp * P : (kp + 1) * P].bitcast(FP8X4),
+                        rhs_scale=x_scales[:, kp * P : (kp + 1) * P],
+                        start=True,
+                        stop=True,
+                    )
+
+        def quantise_hidden(lp):
+            g_grouped = {}
+            for l2 in range(2):
+                g_grouped[l2] = stage.tile([P, ROWS, PACK], BF16, align_bytes=64, tag="g", name="g%d" % l2)
+                for k2, copy_out in ((0, nc.vector.tensor_copy), (1, nc.scalar.copy)):
+                    half = slice(k2 * HALF, (k2 + 1) * HALF)
+                    own_rows = slice(k2 * ROWS, (k2 + 1) * ROWS)
+                    copy_out(
+                        out=g_grouped[l2][half, :, :],
+                        in_=hidden[l2][half, :, own_rows].rearrange("p t b -> p b t"),
+                    )
+            for l2 in range(2):
+                first = (2 * lp + l2) * P
+                nc.vector.quantize_mx(
+                    out=g_codes[:, first : first + ROWS].bitcast(FP8X4),
+                    scales=g_scales[:, first : first + ROWS],
+                    in_=g_grouped[l2][:].rearrange("p b t -> p (b t)"),
+                )
+
+        def second_product(lp):
+            for l in (2 * lp, 2 * lp + 1):
                 nc.tensor.matmul_mx(
-                    out=h_bank[:, kp, :],
-                    lhsT=l_codes[:, cols].bitcast(FP8X4),
-                    lhsT_scale=l_scales[:, cols],
-                    rhs=x_codes[:, kp * P : (kp + 1) * P].bitcast(FP8X4),
-                    rhs_scale=x_scales[:, kp * P : (kp + 1) * P],
+                    out=y[:, l, :],
+                    lhsT=g_codes[:, l * P : (l + 1) * P].bitcast(FP8X4),
+                    lhsT_scale=g_scales[:, l * P : (l + 1) * P],
+                    rhs=r_codes[:, l * S_OUT : (l + 1) * S_OUT].bitcast(FP8X4),
+                    rhs_scale=r_scales[:, l * S_OUT : (l + 1) * S_OUT],
                     start=True,
                     stop=True,
                 )
 
-        def quantise_hidden(l):
-            g_grouped = stage.tile([P, ROWS, PACK], BF16, align_bytes=64)
-            for k2, copy_out in ((0, nc.vector.tensor_copy), (1, nc.scalar.copy)):
-                half = slice(k2 * HALF, (k2 + 1) * HALF)
-                own_rows = slice(k2 * ROWS, (k2 + 1) * ROWS)
-                copy_out(
-                    out=g_grouped[half, :, :],
-                    in_=hidden[l][half, :, own_rows].rearrange("p t b -> p b t"),
-                )
-            nc.vector.quantize_mx(
-                out=g_codes[:, l * P : l * P + ROWS].bitcast(FP8X4),
-                scales=g_scales[:, l * P : l * P + ROWS],
-                in_=g_grouped[:].rearrange("p b t -> p (b t)"),
-            )
-
-        def second_product(l):
-            nc.tensor.matmul_mx(
-                out=y[:, l, :],
-                lhsT=g_codes[:, l * P : (l + 1) * P].bitcast(FP8X4),
-                lhsT_scale=g_scales[:, l * P : (l + 1) * P],
-                rhs=r_codes[:, l * S_OUT : (l + 1) * S_OUT].bitcast(FP8X4),
-                rhs_scale=r_scales[:, l * S_OUT : (l + 1) * S_OUT],
-                start=True,
-                stop=True,
-            )
-
-        for i in range(HEAD_WARM):
-            keep_clock_up()
-        prepare_x()
-        keep_clock_up()
-        for step in range(GROUPS + SECOND_LAG):
-            if step < GROUPS:
-                transpose_and_quantise(step)
-            if step == 1:
-                prepare_factor_r()
-            if step < GROUPS:
-                keep_clock_up()
-            if 0 <= step - FIRST_LAG < GROUPS:
-                first_product(step - FIRST_LAG)
-            if 0 <= step - SECOND_LAG:
-                second_product(step - SECOND_LAG)
-            if 0 <= step - FIRST_LAG < GROUPS:
-                quantise_hidden(step - FIRST_LAG)
+        for lp in range(GROUP_PAIRS):
+            for kp in range(BLOCK_PAIRS):
+                transpose_and_quantise(lp, kp)
+            if lp == 0:
+                prepare_x()
+            if lp >= 1:
+                first_product(lp - 1)
+                quantise_hidden(lp - 1)
+        prepare_factor_r()
+        first_product(GROUP_PAIRS - 1)
+        quantise_hidden(GROUP_PAIRS - 1)
+        for lp in range(GROUP_PAIRS):
+            second_product(lp)
 
         out_rows = keep.tile([ROWS, S_OUT, GROUPS], F32)
         nc.vector.tensor_tensor(

@@ -23,6 +23,10 @@ GROUP_PAIRS = GROUPS // 2
 WORDS = K_PASS // 2
 R_PIECES = GROUPS * S_OUT * PACK // P
 CHUNK = 2 * K_PASS
+CHUNKS = GROUP_PAIRS * BLOCK_PAIRS
+WARM_N = 256
+HEAD_DUMMIES = 6
+LAG = 4
 
 FLOPS = 2 * ROWS * BLOCKS * K_PASS * K_PASS + 2 * ROWS * GROUPS * K_PASS * S_OUT
 
@@ -31,13 +35,18 @@ def tile_butterflyblocksparselinear_s_kernel(tc, x, factorL, factorR, bias, out)
     nc = tc.nc
     with ExitStack() as ctx:
         keep = ctx.enter_context(tc.tile_pool(name="keep", bufs=1))
-        raw_pool = ctx.enter_context(tc.tile_pool(name="raw", bufs=GROUP_PAIRS * BLOCK_PAIRS))
-        stage = ctx.enter_context(tc.tile_pool(name="stage", bufs=2 * BLOCK_PAIRS))
-        code_pool = ctx.enter_context(tc.tile_pool(name="codes", bufs=GROUP_PAIRS * BLOCK_PAIRS))
+        raw_pool = ctx.enter_context(tc.tile_pool(name="raw", bufs=CHUNKS))
+        stage = ctx.enter_context(tc.tile_pool(name="stage", bufs=8))
+        code_pool = ctx.enter_context(tc.tile_pool(name="codes", bufs=CHUNKS))
         flip_pool = ctx.enter_context(tc.psum_pool(name="flip", bufs=5))
         h_pool = ctx.enter_context(tc.psum_pool(name="h", bufs=2))
         y_pool = ctx.enter_context(tc.psum_pool(name="y", bufs=1))
 
+        warm_in = keep.tile([P, WARM_N * PACK], BF16, align_bytes=64)
+        nc.vector.memset(warm_in[:].bitcast(I32), 0)
+        warm_codes = keep.tile([P, WARM_N], U32, align_bytes=64)
+        warm_scales = keep.tile([P, WARM_N], U8, align_bytes=64)
+        nc.vector.quantize_mx(out=warm_codes[:].bitcast(FP8X4), scales=warm_scales[:], in_=warm_in[:])
         ident_f32 = keep.tile([P, P], F32)
         make_identity(nc, ident_f32[:])
         ident_bf16 = keep.tile([P, P], BF16)
@@ -47,106 +56,113 @@ def tile_butterflyblocksparselinear_s_kernel(tc, x, factorL, factorR, bias, out)
         g_scales = keep.tile([P, GROUPS * P], U8, align_bytes=64)
         nc.vector.memset(g_scales[:].bitcast(I32), 0)
 
+        jobs = [("L", 0), ("X", 0), ("L", 1), ("X", 1)]
+        jobs.extend([("L", c) for c in range(2, 12)])
+        jobs.extend([("R", 0), ("R", 1)])
+        jobs.extend([("L", c) for c in range(12, CHUNKS)])
+
         l_rows = factorL.rearrange("k (j l) p -> (k j) (l p)", l=GROUPS)
+        x_rows = x.rearrange("a b (h c) -> (a b h) c", h=2)
         l_raw = {}
-
-        def load_group_pair(lp):
-            for kp in range(BLOCK_PAIRS):
-                chunk = raw_pool.tile([P, CHUNK], BF16)
-                nc.sync.dma_start(
-                    out=chunk[:],
-                    in_=l_rows[kp * P : (kp + 1) * P, lp * CHUNK : (lp + 1) * CHUNK],
-                )
-                l_raw[(lp, kp)] = chunk
-
-        load_group_pair(0)
-        x_raw = keep.tile([P, BLOCKS // 2 * K_PASS], BF16)
-        nc.sync.dma_start(out=x_raw[:], in_=x.rearrange("a b (h c) -> (a b h) c", h=2))
-        load_group_pair(1)
-        load_group_pair(2)
-        load_group_pair(3)
+        x_raw = {}
         r_raw = keep.tile([P, R_PIECES, P], BF16)
-        nc.sync.dma_start(
-            out=r_raw[:],
-            in_=factorR.rearrange("l s (t w) -> (l s t) w", t=PACK).rearrange("(n p) w -> p n w", p=P),
-        )
+        for kind, n in jobs:
+            if kind == "L":
+                lp, kp = divmod(n, BLOCK_PAIRS)
+                chunk = raw_pool.tile([P, CHUNK], BF16)
+                nc.sync.dma_start(out=chunk[:], in_=l_rows[kp * P : (kp + 1) * P, lp * CHUNK : (lp + 1) * CHUNK])
+                l_raw[n] = chunk
+            elif kind == "X":
+                x_half = keep.tile([P, CHUNK], BF16, name="x_raw%d" % n)
+                nc.sync.dma_start(out=x_half[:], in_=x_rows[:, n * CHUNK : (n + 1) * CHUNK])
+                x_raw[n] = x_half
+            elif n == 0:
+                nc.sync.dma_start(
+                    out=r_raw[:],
+                    in_=factorR.rearrange("l s (t w) -> (l s t) w", t=PACK).rearrange("(n p) w -> p n w", p=P),
+                )
         bias_rows = keep.tile([ROWS, GROUPS * S_OUT], BF16)
         nc.sync.dma_start(out=bias_rows[:], in_=bias.partition_broadcast(ROWS))
 
         x_codes = keep.tile([P, BLOCKS * ROWS], U32, align_bytes=64)
         x_scales = keep.tile([P, BLOCKS * ROWS], U8, align_bytes=64)
-
-        def prepare_x():
-            x_words = x_raw[:].bitcast(F32)
-            x_grouped = keep.tile([P, BLOCKS * ROWS * PACK], BF16, align_bytes=64)
-            x_grouped_words = x_grouped[:].bitcast(F32).rearrange(
-                "p (kp k2 b u) -> p kp k2 b u", kp=BLOCK_PAIRS, k2=2, u=2
-            )
-            for i in range(2):
-                x_flip = flip_pool.tile([P, 2, 2, P], F32, tag="flip")
-                for k2 in range(2):
-                    for u in range(2):
-                        first = (2 * i + k2) * WORDS + u * P
-                        nc.tensor.transpose(x_flip[:, k2, u, :], x_words[:, first : first + P], ident_f32[:])
-                by_half = x_flip[:].rearrange("p k2 u (b h) -> p h k2 b u", h=2)
-                copy_out = nc.vector.tensor_copy if i == 0 else nc.scalar.copy
-                for h in range(2):
-                    copy_out(out=x_grouped_words[:, 2 * h + i, :, :, :], in_=by_half[:, h, :, :, :])
-            nc.vector.quantize_mx(out=x_codes[:].bitcast(FP8X4), scales=x_scales[:], in_=x_grouped[:])
-
         r_codes = keep.tile([P, GROUPS * S_OUT], U32, align_bytes=64)
         r_scales = keep.tile([P, GROUPS * S_OUT], U8, align_bytes=64)
-
-        def prepare_factor_r():
-            r_grouped = keep.tile([P, GROUPS * S_OUT * PACK], BF16, align_bytes=64)
-            per_bank = R_PIECES // 2
-            for i in range(2):
-                r_flip = flip_pool.tile([P, per_bank, P], BF16, tag="flip")
-                for n in range(per_bank):
-                    nc.tensor.transpose(r_flip[:, n, :], r_raw[:, i * per_bank + n, :], ident_bf16[:])
-                copy_out = nc.vector.tensor_copy if i == 0 else nc.scalar.copy
-                copy_out(
-                    out=r_grouped[:, i * per_bank * P : (i + 1) * per_bank * P],
-                    in_=r_flip[:].rearrange("p n c -> p (n c)"),
-                )
-            nc.vector.quantize_mx(out=r_codes[:].bitcast(FP8X4), scales=r_scales[:], in_=r_grouped[:])
-
         l_quantised = {}
         hidden = {}
         y = y_pool.tile([P, GROUPS, S_OUT], F32)
 
-        def transpose_and_quantise(lp, kp):
-            raw_words = l_raw[(lp, kp)][:].bitcast(F32)
+        def dummy_pass():
+            nc.tensor.matmul_mx(
+                out=y[:].rearrange("p l s -> p (l s)")[:, 0:WARM_N],
+                lhsT=warm_codes[:, 0:P].bitcast(FP8X4),
+                lhsT_scale=warm_scales[:, 0:P],
+                rhs=warm_codes[:].bitcast(FP8X4),
+                rhs_scale=warm_scales[:],
+                start=True,
+                stop=True,
+            )
+
+        def job_l(c):
+            raw_words = l_raw[c][:].bitcast(F32)
             l_flip = flip_pool.tile([P, 2, 2, P], F32, tag="flip")
             for l2 in range(2):
                 for u in range(2):
                     first = l2 * WORDS + u * P
                     nc.tensor.transpose(l_flip[:, l2, u, :], raw_words[:, first : first + P], ident_f32[:])
-            l_grouped = stage.tile([P, CHUNK], BF16, align_bytes=64)
-            nc.scalar.copy(
+            l_grouped = stage.tile([P, CHUNK], BF16, align_bytes=64, tag="grouped")
+            copy_out = nc.vector.tensor_copy if c % 6 == 4 else nc.scalar.copy
+            copy_out(
                 out=l_grouped[:].bitcast(F32).rearrange("p (l2 c u) -> p l2 c u", l2=2, u=2),
                 in_=l_flip[:].rearrange("p l2 u c -> p l2 c u"),
             )
             l_codes = code_pool.tile([P, 2 * P], U32, align_bytes=64)
             l_scales = code_pool.tile([P, 2 * P], U8, align_bytes=64)
             nc.vector.quantize_mx(out=l_codes[:].bitcast(FP8X4), scales=l_scales[:], in_=l_grouped[:])
-            l_quantised[(lp, kp)] = (l_codes, l_scales)
+            l_quantised[c] = (l_codes, l_scales)
 
-        def first_product(lp):
-            for l2 in range(2):
-                hidden[l2] = h_pool.tile([P, BLOCK_PAIRS, P], F32, tag="h", name="hidden%d" % l2)
-            for kp in range(BLOCK_PAIRS):
-                l_codes, l_scales = l_quantised[(lp, kp)]
+        def job_x(i):
+            x_words = x_raw[i][:].bitcast(F32)
+            x_flip = flip_pool.tile([P, 2, 2, P], F32, tag="flip")
+            for k2 in range(2):
+                for u in range(2):
+                    first = k2 * WORDS + u * P
+                    nc.tensor.transpose(x_flip[:, k2, u, :], x_words[:, first : first + P], ident_f32[:])
+            x_grouped = stage.tile([P, CHUNK], BF16, align_bytes=64, tag="grouped")
+            grouped_words = x_grouped[:].bitcast(F32).rearrange("p (h k2 b u) -> p h k2 b u", h=2, k2=2, u=2)
+            by_half = x_flip[:].rearrange("p k2 u (b h) -> p h k2 b u", h=2)
+            for h in range(2):
+                nc.scalar.copy(out=grouped_words[:, h, :, :, :], in_=by_half[:, h, :, :, :])
+            cols = slice(i * 2 * P, (i + 1) * 2 * P)
+            nc.vector.quantize_mx(out=x_codes[:, cols].bitcast(FP8X4), scales=x_scales[:, cols], in_=x_grouped[:])
+
+        def job_r(i):
+            per_bank = R_PIECES // 2
+            r_flip = flip_pool.tile([P, per_bank, P], BF16, tag="flip")
+            for n in range(per_bank):
+                nc.tensor.transpose(r_flip[:, n, :], r_raw[:, i * per_bank + n, :], ident_bf16[:])
+            r_grouped = stage.tile([P, CHUNK], BF16, align_bytes=64, tag="grouped")
+            nc.vector.tensor_copy(out=r_grouped[:], in_=r_flip[:].rearrange("p n c -> p (n c)"))
+            cols = slice(i * 2 * P, (i + 1) * 2 * P)
+            nc.vector.quantize_mx(out=r_codes[:, cols].bitcast(FP8X4), scales=r_scales[:, cols], in_=r_grouped[:])
+
+        def first_product(c):
+            lp, kp = divmod(c, BLOCK_PAIRS)
+            if kp == 0:
                 for l2 in range(2):
-                    nc.tensor.matmul_mx(
-                        out=hidden[l2][:, kp, :],
-                        lhsT=l_codes[:, l2 * P : (l2 + 1) * P].bitcast(FP8X4),
-                        lhsT_scale=l_scales[:, l2 * P : (l2 + 1) * P],
-                        rhs=x_codes[:, kp * P : (kp + 1) * P].bitcast(FP8X4),
-                        rhs_scale=x_scales[:, kp * P : (kp + 1) * P],
-                        start=True,
-                        stop=True,
-                    )
+                    hidden[l2] = h_pool.tile([P, BLOCK_PAIRS, P], F32, tag="h", name="hidden%d" % l2)
+            l_codes, l_scales = l_quantised[c]
+            x_first = (kp % 2) * 2 * P + (kp // 2) * P
+            for l2 in range(2):
+                nc.tensor.matmul_mx(
+                    out=hidden[l2][:, kp, :],
+                    lhsT=l_codes[:, l2 * P : (l2 + 1) * P].bitcast(FP8X4),
+                    lhsT_scale=l_scales[:, l2 * P : (l2 + 1) * P],
+                    rhs=x_codes[:, x_first : x_first + P].bitcast(FP8X4),
+                    rhs_scale=x_scales[:, x_first : x_first + P],
+                    start=True,
+                    stop=True,
+                )
 
         def quantise_hidden(lp):
             g_grouped = {}
@@ -179,19 +195,29 @@ def tile_butterflyblocksparselinear_s_kernel(tc, x, factorL, factorR, bias, out)
                     stop=True,
                 )
 
-        for lp in range(GROUP_PAIRS):
-            for kp in range(BLOCK_PAIRS):
-                transpose_and_quantise(lp, kp)
-            if lp == 0:
-                prepare_x()
-            if lp >= 1:
-                first_product(lp - 1)
-                quantise_hidden(lp - 1)
-        prepare_factor_r()
-        first_product(GROUP_PAIRS - 1)
-        quantise_hidden(GROUP_PAIRS - 1)
-        for lp in range(GROUP_PAIRS):
-            second_product(lp)
+        def passes_of(job):
+            kind, n = job
+            if kind == "L":
+                first_product(n)
+                if n % BLOCK_PAIRS == BLOCK_PAIRS - 1:
+                    quantise_hidden(n // BLOCK_PAIRS)
+
+        run_job = {"L": job_l, "X": job_x, "R": job_r}
+        with tc.manual_schedule(engines={mybir.EngineType.PE}):
+            for count in range(HEAD_DUMMIES):
+                dummy_pass()
+            for first in range(0, len(jobs) + LAG, 2):
+                for i in (first, first + 1):
+                    if i < len(jobs):
+                        run_job[jobs[i][0]](jobs[i][1])
+                if first + 1 < len(jobs):
+                    dummy_pass()
+                    dummy_pass()
+                for i in (first - LAG, first + 1 - LAG):
+                    if i >= 0:
+                        passes_of(jobs[i])
+            for lp in range(GROUP_PAIRS):
+                second_product(lp)
 
         out_rows = keep.tile([ROWS, S_OUT, GROUPS], F32)
         nc.vector.tensor_tensor(

@@ -24,8 +24,6 @@ WORDS = K_PASS // 2
 R_PIECES = GROUPS * S_OUT * PACK // P
 CHUNK = 2 * K_PASS
 CHUNKS = GROUP_PAIRS * BLOCK_PAIRS
-WARM_N = 256
-HEAD_DUMMIES = 6
 LAG = 4
 
 FLOPS = 2 * ROWS * BLOCKS * K_PASS * K_PASS + 2 * ROWS * GROUPS * K_PASS * S_OUT
@@ -42,11 +40,6 @@ def tile_butterflyblocksparselinear_s_kernel(tc, x, factorL, factorR, bias, out)
         h_pool = ctx.enter_context(tc.psum_pool(name="h", bufs=2))
         y_pool = ctx.enter_context(tc.psum_pool(name="y", bufs=1))
 
-        warm_in = keep.tile([P, WARM_N * PACK], BF16, align_bytes=64)
-        nc.vector.memset(warm_in[:].bitcast(I32), 0)
-        warm_codes = keep.tile([P, WARM_N], U32, align_bytes=64)
-        warm_scales = keep.tile([P, WARM_N], U8, align_bytes=64)
-        nc.vector.quantize_mx(out=warm_codes[:].bitcast(FP8X4), scales=warm_scales[:], in_=warm_in[:])
         ident_f32 = keep.tile([P, P], F32)
         make_identity(nc, ident_f32[:])
         ident_bf16 = keep.tile([P, P], BF16)
@@ -91,17 +84,6 @@ def tile_butterflyblocksparselinear_s_kernel(tc, x, factorL, factorR, bias, out)
         l_quantised = {}
         hidden = {}
         y = y_pool.tile([P, GROUPS, S_OUT], F32)
-
-        def dummy_pass():
-            nc.tensor.matmul_mx(
-                out=y[:].rearrange("p l s -> p (l s)")[:, 0:WARM_N],
-                lhsT=warm_codes[:, 0:P].bitcast(FP8X4),
-                lhsT_scale=warm_scales[:, 0:P],
-                rhs=warm_codes[:].bitcast(FP8X4),
-                rhs_scale=warm_scales[:],
-                start=True,
-                stop=True,
-            )
 
         def job_l(c):
             raw_words = l_raw[c][:].bitcast(F32)
@@ -204,15 +186,10 @@ def tile_butterflyblocksparselinear_s_kernel(tc, x, factorL, factorR, bias, out)
 
         run_job = {"L": job_l, "X": job_x, "R": job_r}
         with tc.manual_schedule(engines={mybir.EngineType.PE}):
-            for count in range(HEAD_DUMMIES):
-                dummy_pass()
             for first in range(0, len(jobs) + LAG, 2):
                 for i in (first, first + 1):
                     if i < len(jobs):
                         run_job[jobs[i][0]](jobs[i][1])
-                if first + 1 < len(jobs):
-                    dummy_pass()
-                    dummy_pass()
                 for i in (first - LAG, first + 1 - LAG):
                     if i >= 0:
                         passes_of(jobs[i])

@@ -21,7 +21,7 @@ S_OUT = 64
 BLOCK_PAIRS = BLOCKS // 2
 GROUP_PAIRS = GROUPS // 2
 WORDS = K_PASS // 2
-R_PIECES = GROUPS * S_OUT * PACK // P
+R_GROUPS = GROUPS // 2
 CHUNK = 2 * K_PASS
 CHUNKS = GROUP_PAIRS * BLOCK_PAIRS
 LAG = 4
@@ -58,7 +58,8 @@ def tile_butterflyblocksparselinear_s_kernel(tc, x, factorL, factorR, bias, out)
         x_rows = x.rearrange("a b (h c) -> (a b h) c", h=2)
         l_raw = {}
         x_raw = {}
-        r_raw = keep.tile([P, R_PIECES, P], BF16)
+        r_rows = factorR.rearrange("l s (a v) -> l (s a) v", a=2)
+        r_raw = {}
         for kind, n in jobs:
             if kind == "L":
                 lp, kp = divmod(n, BLOCK_PAIRS)
@@ -69,11 +70,11 @@ def tile_butterflyblocksparselinear_s_kernel(tc, x, factorL, factorR, bias, out)
                 x_half = keep.tile([P, CHUNK], BF16, name="x_raw%d" % n)
                 nc.sync.dma_start(out=x_half[:], in_=x_rows[:, n * CHUNK : (n + 1) * CHUNK])
                 x_raw[n] = x_half
-            elif n == 0:
-                nc.sync.dma_start(
-                    out=r_raw[:],
-                    in_=factorR.rearrange("l s (t w) -> (l s t) w", t=PACK).rearrange("(n p) w -> p n w", p=P),
-                )
+            else:
+                for l in range(n * R_GROUPS, (n + 1) * R_GROUPS):
+                    r_group = keep.tile([P, 2 * P], BF16, name="r_raw%d" % l)
+                    nc.sync.dma_start(out=r_group[:], in_=r_rows[l])
+                    r_raw[l] = r_group
         bias_rows = keep.tile([ROWS, GROUPS * S_OUT], BF16)
         nc.sync.dma_start(out=bias_rows[:], in_=bias.partition_broadcast(ROWS))
 
@@ -119,12 +120,17 @@ def tile_butterflyblocksparselinear_s_kernel(tc, x, factorL, factorR, bias, out)
             nc.vector.quantize_mx(out=x_codes[:, cols].bitcast(FP8X4), scales=x_scales[:, cols], in_=x_grouped[:])
 
         def job_r(i):
-            per_bank = R_PIECES // 2
-            r_flip = flip_pool.tile([P, per_bank, P], BF16, tag="flip")
-            for n in range(per_bank):
-                nc.tensor.transpose(r_flip[:, n, :], r_raw[:, i * per_bank + n, :], ident_bf16[:])
+            r_flip = flip_pool.tile([P, R_GROUPS, 2, P], BF16, tag="flip")
+            for l4 in range(R_GROUPS):
+                for e in range(2):
+                    nc.tensor.transpose(
+                        r_flip[:, l4, e, :], r_raw[i * R_GROUPS + l4][:, e * P : (e + 1) * P], ident_bf16[:]
+                    )
             r_grouped = stage.tile([P, CHUNK], BF16, align_bytes=64, tag="grouped")
-            nc.vector.tensor_copy(out=r_grouped[:], in_=r_flip[:].rearrange("p n c -> p (n c)"))
+            nc.vector.tensor_copy(
+                out=r_grouped[:].bitcast(F32).rearrange("p (l s e) -> p l s e", l=R_GROUPS, e=2),
+                in_=r_flip[:].bitcast(F32).rearrange("p l e s -> p l s e"),
+            )
             cols = slice(i * 2 * P, (i + 1) * 2 * P)
             nc.vector.quantize_mx(out=r_codes[:, cols].bitcast(FP8X4), scales=r_scales[:, cols], in_=r_grouped[:])
 
@@ -154,8 +160,8 @@ def tile_butterflyblocksparselinear_s_kernel(tc, x, factorL, factorR, bias, out)
                     half = slice(k2 * HALF, (k2 + 1) * HALF)
                     own_rows = slice(k2 * ROWS, (k2 + 1) * ROWS)
                     copy_out(
-                        out=g_grouped[l2][half, :, :],
-                        in_=hidden[l2][half, :, own_rows].rearrange("p t b -> p b t"),
+                        out=g_grouped[l2][half, :, :].rearrange("p b (e a) -> p b e a", a=2),
+                        in_=hidden[l2][half, :, own_rows].rearrange("p (a e) b -> p b e a", a=2),
                     )
             for l2 in range(2):
                 first = (2 * lp + l2) * P
@@ -186,6 +192,7 @@ def tile_butterflyblocksparselinear_s_kernel(tc, x, factorL, factorR, bias, out)
 
         run_job = {"L": job_l, "X": job_x, "R": job_r}
         with tc.manual_schedule(engines={mybir.EngineType.PE}):
+            r_ready = jobs.index(("R", 0)) + LAG
             for first in range(0, len(jobs) + LAG, 2):
                 for i in (first, first + 1):
                     if i < len(jobs):
@@ -193,8 +200,11 @@ def tile_butterflyblocksparselinear_s_kernel(tc, x, factorL, factorR, bias, out)
                 for i in (first - LAG, first + 1 - LAG):
                     if i >= 0:
                         passes_of(jobs[i])
-            for lp in range(GROUP_PAIRS):
-                second_product(lp)
+                for lp in range(GROUP_PAIRS - 1):
+                    last = jobs.index(("L", lp * BLOCK_PAIRS + BLOCK_PAIRS - 1))
+                    if first == max(last + LAG - last % 2 + LAG, r_ready):
+                        second_product(lp)
+            second_product(GROUP_PAIRS - 1)
 
         out_rows = keep.tile([ROWS, S_OUT, GROUPS], F32)
         nc.vector.tensor_tensor(

@@ -21,10 +21,9 @@ S_OUT = 64
 BLOCK_PAIRS = BLOCKS // 2
 GROUP_PAIRS = GROUPS // 2
 WORDS = K_PASS // 2
-R_GROUPS = GROUPS // 2
+R_PARTS = [[0, 1, 2, 3], [4, 5], [6, 7]]
 CHUNK = 2 * K_PASS
 CHUNKS = GROUP_PAIRS * BLOCK_PAIRS
-LAG = 4
 
 FLOPS = 2 * ROWS * BLOCKS * K_PASS * K_PASS + 2 * ROWS * GROUPS * K_PASS * S_OUT
 
@@ -49,10 +48,11 @@ def tile_butterflyblocksparselinear_s_kernel(tc, x, factorL, factorR, bias, out)
         g_scales = keep.tile([P, GROUPS * P], U8, align_bytes=64)
         nc.vector.memset(g_scales[:].bitcast(I32), 0)
 
-        jobs = [("L", 0), ("X", 0), ("L", 1), ("X", 1)]
-        jobs.extend([("L", c) for c in range(2, 12)])
+        jobs = [("X", 0), ("X", 1)]
+        jobs.extend([("L", c) for c in range(0, 12)])
         jobs.extend([("R", 0), ("R", 1)])
         jobs.extend([("L", c) for c in range(12, CHUNKS)])
+        jobs.extend([("R", 2)])
 
         l_rows = factorL.rearrange("k (j l) p -> (k j) (l p)", l=GROUPS)
         x_rows = x.rearrange("a b (h c) -> (a b h) c", h=2)
@@ -71,7 +71,7 @@ def tile_butterflyblocksparselinear_s_kernel(tc, x, factorL, factorR, bias, out)
                 nc.sync.dma_start(out=x_half[:], in_=x_rows[:, n * CHUNK : (n + 1) * CHUNK])
                 x_raw[n] = x_half
             else:
-                for l in range(n * R_GROUPS, (n + 1) * R_GROUPS):
+                for l in R_PARTS[n]:
                     r_group = keep.tile([P, 2 * P], BF16, name="r_raw%d" % l)
                     nc.sync.dma_start(out=r_group[:], in_=r_rows[l])
                     r_raw[l] = r_group
@@ -120,18 +120,18 @@ def tile_butterflyblocksparselinear_s_kernel(tc, x, factorL, factorR, bias, out)
             nc.vector.quantize_mx(out=x_codes[:, cols].bitcast(FP8X4), scales=x_scales[:, cols], in_=x_grouped[:])
 
         def job_r(i):
-            r_flip = flip_pool.tile([P, R_GROUPS, 2, P], BF16, tag="flip")
-            for l4 in range(R_GROUPS):
+            part = R_PARTS[i]
+            r_flip = flip_pool.tile([P, len(part), 2, P], BF16, tag="flip")
+            for n, l in enumerate(part):
                 for e in range(2):
-                    nc.tensor.transpose(
-                        r_flip[:, l4, e, :], r_raw[i * R_GROUPS + l4][:, e * P : (e + 1) * P], ident_bf16[:]
-                    )
-            r_grouped = stage.tile([P, CHUNK], BF16, align_bytes=64, tag="grouped")
-            nc.vector.tensor_copy(
-                out=r_grouped[:].bitcast(F32).rearrange("p (l s e) -> p l s e", l=R_GROUPS, e=2),
+                    nc.tensor.transpose(r_flip[:, n, e, :], r_raw[l][:, e * P : (e + 1) * P], ident_bf16[:])
+            r_grouped = stage.tile([P, len(part) * S_OUT * PACK], BF16, align_bytes=64, tag="grouped")
+            copy_out = nc.scalar.copy if i == len(R_PARTS) - 1 else nc.vector.tensor_copy
+            copy_out(
+                out=r_grouped[:].bitcast(F32).rearrange("p (l s e) -> p l s e", l=len(part), e=2),
                 in_=r_flip[:].bitcast(F32).rearrange("p l e s -> p l s e"),
             )
-            cols = slice(i * 2 * P, (i + 1) * 2 * P)
+            cols = slice(part[0] * S_OUT, (part[-1] + 1) * S_OUT)
             nc.vector.quantize_mx(out=r_codes[:, cols].bitcast(FP8X4), scales=r_scales[:, cols], in_=r_grouped[:])
 
         def first_product(c):
@@ -190,20 +190,30 @@ def tile_butterflyblocksparselinear_s_kernel(tc, x, factorL, factorR, bias, out)
                 if n % BLOCK_PAIRS == BLOCK_PAIRS - 1:
                     quantise_hidden(n // BLOCK_PAIRS)
 
-        run_job = {"L": job_l, "X": job_x, "R": job_r}
+        def transposes_of(lp):
+            for c in range(lp * BLOCK_PAIRS, (lp + 1) * BLOCK_PAIRS):
+                job_l(c)
+
+        def passes_of_pair(lp):
+            for c in range(lp * BLOCK_PAIRS, (lp + 1) * BLOCK_PAIRS):
+                passes_of(("L", c))
+
         with tc.manual_schedule(engines={mybir.EngineType.PE}):
-            r_ready = jobs.index(("R", 0)) + LAG
-            for first in range(0, len(jobs) + LAG, 2):
-                for i in (first, first + 1):
-                    if i < len(jobs):
-                        run_job[jobs[i][0]](jobs[i][1])
-                for i in (first - LAG, first + 1 - LAG):
-                    if i >= 0:
-                        passes_of(jobs[i])
-                for lp in range(GROUP_PAIRS - 1):
-                    last = jobs.index(("L", lp * BLOCK_PAIRS + BLOCK_PAIRS - 1))
-                    if first == max(last + LAG - last % 2 + LAG, r_ready):
-                        second_product(lp)
+            job_x(0)
+            job_x(1)
+            transposes_of(0)
+            transposes_of(1)
+            passes_of_pair(0)
+            transposes_of(2)
+            passes_of_pair(1)
+            job_r(0)
+            job_r(1)
+            passes_of_pair(2)
+            transposes_of(3)
+            for lp in range(GROUP_PAIRS - 1):
+                second_product(lp)
+            job_r(2)
+            passes_of_pair(3)
             second_product(GROUP_PAIRS - 1)
 
         out_rows = keep.tile([ROWS, S_OUT, GROUPS], F32)

@@ -21,7 +21,7 @@ S_OUT = 64
 BLOCK_PAIRS = BLOCKS // 2
 GROUP_PAIRS = GROUPS // 2
 WORDS = K_PASS // 2
-R_PARTS = [[0, 1, 2, 3], [4, 5], [6, 7]]
+R_PARTS = [[0, 1, 2, 3], [4, 5, 6, 7]]
 CHUNK = 2 * K_PASS
 CHUNKS = GROUP_PAIRS * BLOCK_PAIRS
 
@@ -50,9 +50,8 @@ def tile_butterflyblocksparselinear_s_kernel(tc, x, factorL, factorR, bias, out)
 
         jobs = [("X", 0), ("X", 1)]
         jobs.extend([("L", c) for c in range(0, 12)])
-        jobs.extend([("R", 0), ("R", 1)])
         jobs.extend([("L", c) for c in range(12, CHUNKS)])
-        jobs.extend([("R", 2)])
+        jobs.extend([("R", 0), ("R", 1)])
 
         l_rows = factorL.rearrange("k (j l) p -> (k j) (l p)", l=GROUPS)
         x_rows = x.rearrange("a b (h c) -> (a b h) c", h=2)
@@ -126,7 +125,7 @@ def tile_butterflyblocksparselinear_s_kernel(tc, x, factorL, factorR, bias, out)
                 for e in range(2):
                     nc.tensor.transpose(r_flip[:, n, e, :], r_raw[l][:, e * P : (e + 1) * P], ident_bf16[:])
             r_grouped = stage.tile([P, len(part) * S_OUT * PACK], BF16, align_bytes=64, tag="grouped")
-            copy_out = nc.scalar.copy if i == len(R_PARTS) - 1 else nc.vector.tensor_copy
+            copy_out = nc.scalar.copy
             copy_out(
                 out=r_grouped[:].bitcast(F32).rearrange("p (l s e) -> p l s e", l=len(part), e=2),
                 in_=r_flip[:].bitcast(F32).rearrange("p l e s -> p l s e"),
@@ -206,15 +205,13 @@ def tile_butterflyblocksparselinear_s_kernel(tc, x, factorL, factorR, bias, out)
             passes_of_pair(0)
             transposes_of(2)
             passes_of_pair(1)
+            transposes_of(3)
+            passes_of_pair(2)
             job_r(0)
             job_r(1)
-            passes_of_pair(2)
-            transposes_of(3)
-            for lp in range(GROUP_PAIRS - 1):
-                second_product(lp)
-            job_r(2)
             passes_of_pair(3)
-            second_product(GROUP_PAIRS - 1)
+            for lp in range(GROUP_PAIRS):
+                second_product(lp)
 
         out_rows = keep.tile([ROWS, S_OUT, GROUPS], F32)
         nc.vector.tensor_tensor(

@@ -155,7 +155,8 @@ def tile_butterflyblocksparselinear_s_kernel(tc, x, factorL, factorR, bias, out)
             g_grouped = {}
             for l2 in range(2):
                 g_grouped[l2] = stage.tile([P, ROWS, PACK], BF16, align_bytes=64, tag="g", name="g%d" % l2)
-                for k2, copy_out in ((0, nc.vector.tensor_copy), (1, nc.scalar.copy)):
+                upper = nc.scalar.copy if lp == GROUP_PAIRS - 2 else nc.vector.tensor_copy
+                for k2, copy_out in ((0, upper), (1, nc.scalar.copy)):
                     half = slice(k2 * HALF, (k2 + 1) * HALF)
                     own_rows = slice(k2 * ROWS, (k2 + 1) * ROWS)
                     copy_out(
@@ -197,21 +198,20 @@ def tile_butterflyblocksparselinear_s_kernel(tc, x, factorL, factorR, bias, out)
             for c in range(lp * BLOCK_PAIRS, (lp + 1) * BLOCK_PAIRS):
                 passes_of(("L", c))
 
-        with tc.manual_schedule(engines={mybir.EngineType.PE}):
-            job_x(0)
-            job_x(1)
-            transposes_of(0)
-            transposes_of(1)
-            passes_of_pair(0)
-            transposes_of(2)
-            passes_of_pair(1)
-            transposes_of(3)
-            passes_of_pair(2)
-            job_r(0)
-            job_r(1)
-            passes_of_pair(3)
-            for lp in range(GROUP_PAIRS):
-                second_product(lp)
+        job_x(0)
+        job_x(1)
+        transposes_of(0)
+        transposes_of(1)
+        passes_of_pair(0)
+        transposes_of(2)
+        passes_of_pair(1)
+        transposes_of(3)
+        passes_of_pair(2)
+        job_r(0)
+        job_r(1)
+        passes_of_pair(3)
+        for lp in range(GROUP_PAIRS):
+            second_product(lp)
 
         out_rows = keep.tile([ROWS, S_OUT, GROUPS], F32)
         nc.vector.tensor_tensor(

from contextlib import ExitStack

import concourse.mybir as mybir
from concourse.masks import make_identity

FP8X4 = mybir.dt.float8_e4m3fn_x4
BF16 = mybir.dt.bfloat16
F32 = mybir.dt.float32
I32 = mybir.dt.int32
U32 = mybir.dt.uint32
U8 = mybir.dt.uint8

P = 128
HALF = P // 2
PACK = 4
ROWS = 64
K_PASS = 512
BLOCKS = 8
GROUPS = 8
S_OUT = 64
BLOCK_PAIRS = BLOCKS // 2
GROUP_PAIRS = GROUPS // 2
WORDS = K_PASS // 2
R_PARTS = [[0, 1, 2, 3], [4, 5, 6, 7]]
CHUNK = 2 * K_PASS
CHUNKS = GROUP_PAIRS * BLOCK_PAIRS

FLOPS = 2 * ROWS * BLOCKS * K_PASS * K_PASS + 2 * ROWS * GROUPS * K_PASS * S_OUT


def tile_butterflyblocksparselinear_s_kernel(tc, x, factorL, factorR, bias, out):
    nc = tc.nc
    with ExitStack() as ctx:
        keep = ctx.enter_context(tc.tile_pool(name="keep", bufs=1))
        raw_pool = ctx.enter_context(tc.tile_pool(name="raw", bufs=CHUNKS))
        stage = ctx.enter_context(tc.tile_pool(name="stage", bufs=8))
        code_pool = ctx.enter_context(tc.tile_pool(name="codes", bufs=CHUNKS))
        flip_pool = ctx.enter_context(tc.psum_pool(name="flip", bufs=5))
        h_pool = ctx.enter_context(tc.psum_pool(name="h", bufs=2))
        y_pool = ctx.enter_context(tc.psum_pool(name="y", bufs=1))

        ident_f32 = keep.tile([P, P], F32)
        make_identity(nc, ident_f32[:])
        ident_bf16 = keep.tile([P, P], BF16)
        make_identity(nc, ident_bf16[:])
        g_codes = keep.tile([P, GROUPS * P], U32, align_bytes=64)
        nc.vector.memset(g_codes[:].bitcast(I32), 0)
        g_scales = keep.tile([P, GROUPS * P], U8, align_bytes=64)
        nc.vector.memset(g_scales[:].bitcast(I32), 0)

        jobs = [("X", 0), ("X", 1)]
        jobs.extend([("L", c) for c in range(0, 12)])
        jobs.extend([("L", c) for c in range(12, CHUNKS)])
        jobs.extend([("R", 0), ("R", 1)])

        l_rows = factorL.rearrange("k (j l) p -> (k j) (l p)", l=GROUPS)
        x_rows = x.rearrange("a b (h c) -> (a b h) c", h=2)
        l_raw = {}
        x_raw = {}
        r_rows = factorR.rearrange("l s (a v) -> l (s a) v", a=2)
        r_raw = {}
        for kind, n in jobs:
            if kind == "L":
                lp, kp = divmod(n, BLOCK_PAIRS)
                chunk = raw_pool.tile([P, CHUNK], BF16)
                nc.sync.dma_start(out=chunk[:], in_=l_rows[kp * P : (kp + 1) * P, lp * CHUNK : (lp + 1) * CHUNK])
                l_raw[n] = chunk
            elif kind == "X":
                x_half = keep.tile([P, CHUNK], BF16, name="x_raw%d" % n)
                nc.sync.dma_start(out=x_half[:], in_=x_rows[:, n * CHUNK : (n + 1) * CHUNK])
                x_raw[n] = x_half
            else:
                for l in R_PARTS[n]:
                    r_group = keep.tile([P, 2 * P], BF16, name="r_raw%d" % l)
                    nc.sync.dma_start(out=r_group[:], in_=r_rows[l])
                    r_raw[l] = r_group
        bias_rows = keep.tile([ROWS, GROUPS * S_OUT], BF16)
        nc.sync.dma_start(out=bias_rows[:], in_=bias.partition_broadcast(ROWS))

        x_codes = keep.tile([P, BLOCKS * ROWS], U32, align_bytes=64)
        x_scales = keep.tile([P, BLOCKS * ROWS], U8, align_bytes=64)
        r_codes = keep.tile([P, GROUPS * S_OUT], U32, align_bytes=64)
        r_scales = keep.tile([P, GROUPS * S_OUT], U8, align_bytes=64)
        l_quantised = {}
        hidden = {}
        y = y_pool.tile([P, GROUPS, S_OUT], F32)

        def job_l(c):
            raw_words = l_raw[c][:].bitcast(F32)
            l_flip = flip_pool.tile([P, 2, 2, P], F32, tag="flip")
            for l2 in range(2):
                for u in range(2):
                    first = l2 * WORDS + u * P
                    nc.tensor.transpose(l_flip[:, l2, u, :], raw_words[:, first : first + P], ident_f32[:])
            l_grouped = stage.tile([P, CHUNK], BF16, align_bytes=64, tag="grouped")
            copy_out = nc.vector.tensor_copy if c % 6 == 4 else nc.scalar.copy
            copy_out(
                out=l_grouped[:].bitcast(F32).rearrange("p (l2 c u) -> p l2 c u", l2=2, u=2),
                in_=l_flip[:].rearrange("p l2 u c -> p l2 c u"),
            )
            l_codes = code_pool.tile([P, 2 * P], U32, align_bytes=64)
            l_scales = code_pool.tile([P, 2 * P], U8, align_bytes=64)
            nc.vector.quantize_mx(out=l_codes[:].bitcast(FP8X4), scales=l_scales[:], in_=l_grouped[:])
            l_quantised[c] = (l_codes, l_scales)

        def job_x(i):
            x_words = x_raw[i][:].bitcast(F32)
            x_flip = flip_pool.tile([P, 2, 2, P], F32, tag="flip")
            for k2 in range(2):
                for u in range(2):
                    first = k2 * WORDS + u * P
                    nc.tensor.transpose(x_flip[:, k2, u, :], x_words[:, first : first + P], ident_f32[:])
            x_grouped = stage.tile([P, CHUNK], BF16, align_bytes=64, tag="grouped")
            grouped_words = x_grouped[:].bitcast(F32).rearrange("p (h k2 b u) -> p h k2 b u", h=2, k2=2, u=2)
            by_half = x_flip[:].rearrange("p k2 u (b h) -> p h k2 b u", h=2)
            for h in range(2):
                nc.scalar.copy(out=grouped_words[:, h, :, :, :], in_=by_half[:, h, :, :, :])
            cols = slice(i * 2 * P, (i + 1) * 2 * P)
            nc.vector.quantize_mx(out=x_codes[:, cols].bitcast(FP8X4), scales=x_scales[:, cols], in_=x_grouped[:])

        def job_r(i):
            part = R_PARTS[i]
            r_flip = flip_pool.tile([P, len(part), 2, P], BF16, tag="flip")
            for n, l in enumerate(part):
                for e in range(2):
                    nc.tensor.transpose(r_flip[:, n, e, :], r_raw[l][:, e * P : (e + 1) * P], ident_bf16[:])
            r_grouped = stage.tile([P, len(part) * S_OUT * PACK], BF16, align_bytes=64, tag="grouped")
            copy_out = nc.scalar.copy
            copy_out(
                out=r_grouped[:].bitcast(F32).rearrange("p (l s e) -> p l s e", l=len(part), e=2),
                in_=r_flip[:].bitcast(F32).rearrange("p l e s -> p l s e"),
            )
            cols = slice(part[0] * S_OUT, (part[-1] + 1) * S_OUT)
            nc.vector.quantize_mx(out=r_codes[:, cols].bitcast(FP8X4), scales=r_scales[:, cols], in_=r_grouped[:])

        def first_product(c):
            lp, kp = divmod(c, BLOCK_PAIRS)
            if kp == 0:
                for l2 in range(2):
                    hidden[l2] = h_pool.tile([P, BLOCK_PAIRS, P], F32, tag="h", name="hidden%d" % l2)
            l_codes, l_scales = l_quantised[c]
            x_first = (kp % 2) * 2 * P + (kp // 2) * P
            for l2 in range(2):
                nc.tensor.matmul_mx(
                    out=hidden[l2][:, kp, :],
                    lhsT=l_codes[:, l2 * P : (l2 + 1) * P].bitcast(FP8X4),
                    lhsT_scale=l_scales[:, l2 * P : (l2 + 1) * P],
                    rhs=x_codes[:, x_first : x_first + P].bitcast(FP8X4),
                    rhs_scale=x_scales[:, x_first : x_first + P],
                    start=True,
                    stop=True,
                )

        def quantise_hidden(lp):
            g_grouped = {}
            for l2 in range(2):
                g_grouped[l2] = stage.tile([P, ROWS, PACK], BF16, align_bytes=64, tag="g", name="g%d" % l2)
                upper = nc.scalar.copy if lp == GROUP_PAIRS - 2 else nc.vector.tensor_copy
                for k2, copy_out in ((0, upper), (1, nc.scalar.copy)):
                    half = slice(k2 * HALF, (k2 + 1) * HALF)
                    own_rows = slice(k2 * ROWS, (k2 + 1) * ROWS)
                    copy_out(
                        out=g_grouped[l2][half, :, :].rearrange("p b (e a) -> p b e a", a=2),
                        in_=hidden[l2][half, :, own_rows].rearrange("p (a e) b -> p b e a", a=2),
                    )
            for l2 in range(2):
                first = (2 * lp + l2) * P
                nc.vector.quantize_mx(
                    out=g_codes[:, first : first + ROWS].bitcast(FP8X4),
                    scales=g_scales[:, first : first + ROWS],
                    in_=g_grouped[l2][:].rearrange("p b t -> p (b t)"),
                )

        def second_product(lp):
            for l in (2 * lp, 2 * lp + 1):
                nc.tensor.matmul_mx(
                    out=y[:, l, :],
                    lhsT=g_codes[:, l * P : (l + 1) * P].bitcast(FP8X4),
                    lhsT_scale=g_scales[:, l * P : (l + 1) * P],
                    rhs=r_codes[:, l * S_OUT : (l + 1) * S_OUT].bitcast(FP8X4),
                    rhs_scale=r_scales[:, l * S_OUT : (l + 1) * S_OUT],
                    start=True,
                    stop=True,
                )

        def passes_of(job):
            kind, n = job
            if kind == "L":
                first_product(n)
                if n % BLOCK_PAIRS == BLOCK_PAIRS - 1:
                    quantise_hidden(n // BLOCK_PAIRS)

        def transposes_of(lp):
            for c in range(lp * BLOCK_PAIRS, (lp + 1) * BLOCK_PAIRS):
                job_l(c)

        def passes_of_pair(lp):
            for c in range(lp * BLOCK_PAIRS, (lp + 1) * BLOCK_PAIRS):
                passes_of(("L", c))

        job_x(0)
        job_x(1)
        transposes_of(0)
        transposes_of(1)
        passes_of_pair(0)
        transposes_of(2)
        passes_of_pair(1)
        transposes_of(3)
        passes_of_pair(2)
        job_r(0)
        job_r(1)
        passes_of_pair(3)
        for lp in range(GROUP_PAIRS):
            second_product(lp)

        out_rows = keep.tile([ROWS, S_OUT, GROUPS], F32)
        nc.vector.tensor_tensor(
            out=out_rows[:],
            in0=y[0:ROWS, :, :].rearrange("b l s -> b s l"),
            in1=bias_rows[:].rearrange("b (s l) -> b s l", l=GROUPS),
            op=mybir.AluOpType.add,
        )
        nc.sync.dma_start(
            out=out.rearrange("a b n -> (a b) n"),
            in_=out_rows[:].rearrange("b s l -> b (s l)"),
        )
